import numpy as np
import ml_dtypes


def mxq(x, axis, fmt="e4m3"):
    dtype, down = {"e4m3": (ml_dtypes.float8_e4m3fn, 7), "e5m2": (ml_dtypes.float8_e5m2, 14)}[fmt]
    v = np.moveaxis(np.asarray(x, np.float32).astype(ml_dtypes.bfloat16).astype(np.float64), axis, -1)
    blocks = v.reshape(v.shape[:-1] + (-1, 32))
    amax = np.abs(blocks).max(-1, keepdims=True)
    byte = np.maximum(np.where(amax > 0, np.frexp(amax)[1] - 1 + 127, 0) - down, 1)
    scale = np.exp2(byte - 127.0)
    codes = (blocks / scale).astype(np.float32).astype(dtype).astype(np.float64)
    return np.moveaxis((codes * scale).reshape(v.shape), -1, axis)


WIDE = False


def mx_kscale(k):
    if not WIDE:
        return np.ones(k)
    levels = np.array([10, -10, 5, -5, 0])
    a = np.random.permutation(np.resize(levels, k // 512 * 4)).reshape(k // 512, 4)
    idx = np.arange(k)
    return np.exp2(a[idx // 512, idx % 128 // 32])


BF16 = ml_dtypes.bfloat16


def bf(x):
    return np.asarray(x, np.float32).astype(BF16)


def f64(x):
    return np.asarray(x).astype(np.float64)


E2M1 = np.array([0.0, 0.5, 1.0, 1.5, 2.0, 3.0, 4.0, 6.0, -0.0, -0.5, -1.0, -1.5, -2.0, -3.0, -4.0, -6.0])


def pack_weight(w, fmt):
    k, n = w.shape
    w = f64(bf(w)).reshape(k // 32, 32, n)
    amax = np.abs(w).max(1)
    if fmt == "e4m3":
        byte = np.frexp(amax)[1] - 1 + 127 - 7
    else:
        mant, ex = np.frexp(amax / 6.0)
        byte = np.where(mant > 0.5, ex, ex - 1) + 127
    byte = np.clip(np.where(amax > 0, byte, 1), 1, 254)
    scaled = (w * np.exp2(127.0 - byte)[:, None, :]).reshape(k, n).astype(np.float32)
    by_word = np.ascontiguousarray(scaled.reshape(k // 512, 128, 4, n).transpose(0, 1, 3, 2))
    if fmt == "e4m3":
        words = by_word.astype(ml_dtypes.float8_e4m3fn).view(np.uint8)
    else:
        c = by_word.astype(ml_dtypes.float4_e2m1fn).view(np.uint8) & 0xF
        words = c[..., 0::2] | (c[..., 1::2] << 4)
    return np.ascontiguousarray(words), np.ascontiguousarray(byte.astype(np.uint8).reshape(k // 512, 16, n))


def unpack_weight(words, scales, fmt):
    g, p, n, _ = words.shape
    if fmt == "e4m3":
        vals = np.ascontiguousarray(words).view(ml_dtypes.float8_e4m3fn).astype(np.float64)
    else:
        nib = np.empty((g, p, n, 4), np.uint8)
        nib[..., 0::2] = words & 0xF
        nib[..., 1::2] = words >> 4
        vals = E2M1[nib]
    vals = vals * np.repeat(np.exp2(scales.astype(np.float64) - 127.0), 8, axis=1)[..., None]
    return vals.transpose(0, 1, 3, 2).reshape(g * 512, n)

def pack4(w):
    words, scales = pack_weight(w, "e2m1")
    return words.reshape(words.shape[0], 128, -1), scales


def unpack4(words, scales):
    return unpack_weight(words.reshape(words.shape[0], 128, -1, 2), scales, "e2m1")


B, HW, C, HID, WS, SS, HEADS = 1, 16, 1024, 2048, 8, 4, 16
L = HW * HW
NH = HW // WS
EPS = 1e-5


def adain(x, scale, shift):
    m = x.mean(2, keepdims=True)
    s = np.std(x, axis=2, keepdims=True, ddof=1) + EPS
    return (x - m) / s * scale + shift


def setup_inputs():
    s = mx_kscale(C)
    o_attn = bf(0.4 * np.random.standard_normal((NH * NH * B, WS * WS, C)) * s)
    out_w = np.random.standard_normal((C, C)) / np.sqrt(C) / s[None, :]
    words, scales = pack4(np.ascontiguousarray(out_w.T))
    return {"o_attn": o_attn,
            "out_w_words": words,
            "out_w_scales": scales,
            "out_b": bf(0.1 * np.random.standard_normal(C)),
            "ada1_scale": bf(1.0 + 0.1 * np.random.standard_normal((1, L, 1))),
            "ada1_shift": bf(0.1 * np.random.standard_normal((1, L, 1))),
            "x": bf(np.random.standard_normal((B, L, C)))}


def reference(o_attn, out_w_words, out_w_scales, out_b, ada1_scale, ada1_shift, x):
    a = (mxq(f64(o_attn), 2, "e4m3") @ unpack4(out_w_words, out_w_scales)) + f64(out_b)
    a = np.swapaxes(a.reshape(B, NH, NH, WS, WS, C), 2, 3).reshape(B, HW, HW, C)
    a = np.roll(a, (SS, SS), axis=(1, 2)).reshape(B, L, C)
    return f64(x) + adain(a, f64(ada1_scale), f64(ada1_shift))

@@ -1,0 +1,297 @@
+from contextlib import ExitStack
+
+import concourse.mybir as mybir
+from concourse.masks import make_identity
+
+F32 = mybir.dt.float32
+BF16 = mybir.dt.bfloat16
+I32 = mybir.dt.int32
+U32 = mybir.dt.uint32
+U8 = mybir.dt.uint8
+FP8X4 = mybir.dt.float8_e4m3fn_x4
+FP4X4 = mybir.dt.float4_e2m1fn_x4
+ALU = mybir.AluOpType
+ACT = mybir.ActivationFunctionType
+
+P = 128
+GRID = 16
+WIN = 8
+SHIFT = 4
+TOKENS = GRID * GRID
+CHANNELS = 1024
+EPS = 1e-5
+
+TILES = TOKENS // P
+K_PASS = 4 * P
+PASSES = CHANNELS // K_PASS
+BANK = 512
+BANKS = CHANNELS // BANK
+
+WARM = 4
+
+FLOPS = 2 * TOKENS * CHANNELS * CHANNELS
+
+
+def token_runs(s):
+    first = P * s + SHIFT * GRID
+    if first + P <= TOKENS:
+        return [(0, first, P)]
+    head = TOKENS - first
+    return [(0, first, head), (head, 0, P - head)]
+
+
+def tile_swintransformerblock_pb_s_kernel(
+    tc, o_attn, out_w_words, out_w_scales, out_b, ada1_scale, ada1_shift, x, out
+):
+    nc = tc.nc
+    with ExitStack() as ctx:
+        keep = ctx.enter_context(tc.tile_pool(name="keep", bufs=1))
+        psum = ctx.enter_context(tc.psum_pool(name="psum", bufs=1))
+        ctx.enter_context(tc.manual_schedule())
+
+        def one_per_tile(pool, shape, dtype, name, align_bytes=None):
+            return [
+                pool.tile(shape, dtype, name="%s%d" % (name, s), align_bytes=align_bytes)
+                for s in range(TILES)
+            ]
+
+        tile_order = [1, 0]
+
+        warm_src = keep.tile([P, P], F32)
+        nc.vector.memset(warm_src[:], 1.0)
+        warm_ps = psum.tile([P, WARM, P], F32, name="warm_ps", tag="acc%d%d" % (tile_order[1], 0))
+        for i in range(WARM):
+            nc.tensor.matmul(
+                out=warm_ps[:, i, :], lhsT=warm_src[:], rhs=warm_src[:], start=True, stop=True
+            )
+
+        bias_rows = keep.tile([P, CHANNELS], BF16)
+        nc.vector.memset(bias_rows[:].bitcast(I32), 0)
+        nc.scalar.dma_start(out=bias_rows[0:1, :], in_=out_b.rearrange("(o c) -> o c", o=1))
+
+        o_rows = o_attn.rearrange("w t c -> (w t) c")
+        o_sb = one_per_tile(keep, [P, CHANNELS], BF16, "o_sb")
+        for s in tile_order:
+            nc.sync.dma_start(out=o_sb[s][:], in_=o_rows[P * s : P * (s + 1), :])
+
+        w_words = [
+            keep.tile([P, PASSES, 2 * BANK], U8, name="w_words%d" % h, align_bytes=64)
+            for h in range(BANKS)
+        ]
+
+        def load_w_words(h):
+            nc.sync.dma_start(
+                out=w_words[h][:].bitcast(I32),
+                in_=out_w_words.rearrange("g p b -> p g b")[
+                    :, :, 2 * BANK * h : 2 * BANK * (h + 1)
+                ].bitcast(I32),
+            )
+
+        w_scales = keep.tile([P, PASSES, CHANNELS], U8, align_bytes=64)
+        nc.vector.memset(w_scales[:].bitcast(I32), 0)
+        for r in range(4):
+            nc.sync.dma_start(
+                out=w_scales[r:P:32, :, :].bitcast(I32),
+                in_=out_w_scales[:, r:16:4, :].rearrange("g q n -> q g n").bitcast(I32),
+            )
+        load_w_words(0)
+        load_w_words(1)
+
+        x_sb = one_per_tile(keep, [P, CHANNELS], BF16, "x_sb")
+        gain_bf = one_per_tile(keep, [P, 1], BF16, "gain_bf")
+        offset_bf = one_per_tile(keep, [P, 1], BF16, "offset_bf")
+        for s in tile_order:
+            for p0, t0, count in token_runs(s):
+                nc.sync.dma_start(out=x_sb[s][p0 : p0 + count, :], in_=x[0, t0 : t0 + count, :])
+            with nc.allow_non_contiguous_dma(reason="one 2-byte value for each partition"):
+                for p0, t0, count in token_runs(s):
+                    nc.sync.dma_start(
+                        out=offset_bf[s][p0 : p0 + count, :], in_=ada1_shift[0, t0 : t0 + count, :]
+                    )
+        for s in tile_order:
+            with nc.allow_non_contiguous_dma(reason="one 2-byte value for each partition"):
+                for p0, t0, count in token_runs(s):
+                    nc.sync.dma_start(
+                        out=gain_bf[s][p0 : p0 + count, :], in_=ada1_scale[0, t0 : t0 + count, :]
+                    )
+
+        ones = keep.tile([P, P], BF16)
+        nc.vector.memset(ones[:], 1.0)
+        one_col = keep.tile([P, 1], F32)
+        nc.vector.memset(one_col[:], 1.0)
+        sqrt_warm = keep.tile([P, 1], F32)
+        nc.scalar.activation(out=sqrt_warm[:], in_=one_col[:], func=ACT.Sqrt)
+
+        ident = keep.tile([P, P], F32)
+        make_identity(nc, ident[:])
+        perm = keep.tile([P, P], F32)
+        by_window = ident[:].rearrange("p (wj r c) -> p wj r c", wj=2, r=WIN)
+        by_image_row = perm[:].rearrange("p (r j) -> p r j", j=GRID)
+        nc.vector.tensor_copy(out=by_image_row[:, :, SHIFT : SHIFT + WIN], in_=by_window[:, 0, :, :])
+        nc.vector.tensor_copy(
+            out=by_image_row[:, :, SHIFT + WIN : GRID], in_=by_window[:, 1, :, 0 : WIN - SHIFT]
+        )
+        nc.vector.tensor_copy(out=by_image_row[:, :, 0:SHIFT], in_=by_window[:, 1, :, WIN - SHIFT : WIN])
+
+        def per_pass(pool, shape, dtype, name, align_bytes=None):
+            return [
+                [
+                    pool.tile(shape, dtype, name="%s%d%d" % (name, s, g), align_bytes=align_bytes)
+                    for g in range(PASSES)
+                ]
+                for s in range(TILES)
+            ]
+
+        transposed = per_pass(psum, [P, 4, P], F32, "transposed")
+        grouped = per_pass(keep, [P, P * 4], BF16, "grouped", align_bytes=64)
+        a_words = per_pass(keep, [P, P], U32, "a_words", align_bytes=64)
+        a_scales = per_pass(keep, [P, P], U8, "a_scales", align_bytes=64)
+
+        def transpose_and_copy(s):
+            o_pairs = o_sb[s][:].bitcast(F32)
+            for g in range(PASSES):
+                for u in range(2):
+                    nc.tensor.transpose(
+                        transposed[s][g][:, u, :],
+                        o_pairs[:, 2 * P * g + u : 2 * P * (g + 1) : 2],
+                        perm[:],
+                    )
+            for g in range(PASSES):
+                nc.scalar.copy(
+                    out=grouped[s][g][:].bitcast(F32).rearrange("p (n u) -> p n u", u=2),
+                    in_=transposed[s][g][:, 0:2, :].rearrange("p u n -> p n u"),
+                )
+
+        def quantise(s, g):
+            nc.vector.quantize_mx(
+                out=a_words[s][g][:].bitcast(FP8X4), scales=a_scales[s][g][:], in_=grouped[s][g][:]
+            )
+
+        acc = [[None for h in range(BANKS)] for s in range(TILES)]
+
+        def project(s, h):
+            acc[s][h] = psum.tile([P, BANK], F32, name="acc%d%d" % (s, h), tag="acc%d%d" % (s, h))
+            for g in range(PASSES):
+                nc.tensor.matmul_mx(
+                    out=acc[s][h][:],
+                    lhsT=a_words[s][g][:].bitcast(FP8X4),
+                    lhsT_scale=a_scales[s][g][:],
+                    rhs=w_words[h][:, g, :].bitcast(FP4X4),
+                    rhs_scale=w_scales[:, g, BANK * h : BANK * (h + 1)],
+                    start=(g == 0),
+                    stop=(g == PASSES - 1),
+                )
+
+        a_sb = one_per_tile(keep, [P, CHANNELS], F32, "a_sb")
+        row_sums = one_per_tile(keep, [P, BANKS], F32, "row_sums")
+
+        def add_bias(s, h):
+            cols = slice(BANK * h, BANK * (h + 1))
+            nc.vector.scalar_tensor_tensor(
+                out=a_sb[s][:, cols],
+                in0=acc[s][h][:],
+                scalar=1.0,
+                in1=bias_all[:, cols],
+                op0=ALU.mult,
+                op1=ALU.add,
+                accum_out=row_sums[s][:, h : h + 1],
+            )
+
+        first, last = tile_order
+        transpose_and_copy(first)
+        bias_ps = psum.tile([P, CHANNELS], BF16, name="bias_ps", tag="acc%d%d" % (last, BANKS - 1))
+        for h in range(BANKS):
+            cols = slice(BANK * h, BANK * (h + 1))
+            nc.tensor.matmul(
+                out=bias_ps[:, cols], lhsT=ones[:], rhs=bias_rows[:, cols], start=True, stop=True
+            )
+        transpose_and_copy(last)
+        quantise(first, 0)
+        quantise(first, 1)
+        bias_all = keep.tile([P, CHANNELS], BF16)
+        nc.vector.tensor_copy(out=bias_all[:], in_=bias_ps[:])
+        quantise(last, 0)
+        project(first, 0)
+        add_bias(first, 0)
+        quantise(last, 1)
+        project(first, 1)
+        project(last, 0)
+        project(last, 1)
+
+        x_offset = one_per_tile(keep, [P, CHANNELS], F32, "x_offset")
+        gain = one_per_tile(keep, [P, 1], F32, "gain")
+        nc.scalar.activation(
+            out=x_offset[tile_order[0]][:],
+            in_=x_sb[tile_order[0]][:],
+            func=ACT.Identity,
+            bias=offset_bf[tile_order[0]][:],
+            scale=1.0,
+        )
+        nc.gpsimd.tensor_scalar(
+            out=x_offset[tile_order[1]][:],
+            in0=x_sb[tile_order[1]][:],
+            scalar1=1.0,
+            scalar2=offset_bf[tile_order[1]][:],
+            op0=ALU.mult,
+            op1=ALU.add,
+        )
+
+        neg_mean = one_per_tile(keep, [P, 1], F32, "neg_mean")
+        squares = one_per_tile(keep, [P, CHANNELS], F32, "squares")
+        sum_squares = one_per_tile(keep, [P, 1], F32, "sum_squares")
+        centred = one_per_tile(keep, [P, CHANNELS], F32, "centred")
+        std = one_per_tile(keep, [P, 1], F32, "std")
+        for s in tile_order:
+            for h in range(BANKS):
+                if (s, h) != (first, 0):
+                    add_bias(s, h)
+            nc.vector.tensor_scalar(
+                out=neg_mean[s][:],
+                in0=row_sums[s][:, 0:1],
+                scalar1=row_sums[s][:, 1:2],
+                scalar2=-1.0 / CHANNELS,
+                op0=ALU.add,
+                op1=ALU.mult,
+            )
+            nc.scalar.activation(
+                out=squares[s][:],
+                in_=a_sb[s][:],
+                func=ACT.Square,
+                bias=neg_mean[s][:],
+                scale=1.0,
+                accum_out=sum_squares[s][:],
+            )
+            nc.scalar.activation(
+                out=std[s][:], in_=sum_squares[s][:], func=ACT.Sqrt, scale=1.0 / (CHANNELS - 1)
+            )
+            centring_engine = nc.gpsimd if s == tile_order[0] else nc.vector
+            centring_engine.tensor_copy(out=gain[s][:], in_=gain_bf[s][:])
+            centring_engine.tensor_scalar(
+                out=centred[s][:],
+                in0=a_sb[s][:],
+                scalar1=neg_mean[s][:],
+                scalar2=gain[s][:],
+                op0=ALU.add,
+                op1=ALU.mult,
+            )
+
+        std_eps = one_per_tile(keep, [P, 1], F32, "std_eps")
+        inv_std = one_per_tile(keep, [P, 1], F32, "inv_std")
+        result = one_per_tile(keep, [P, CHANNELS], F32, "result")
+        for s in tile_order:
+            nc.vector.tensor_scalar_add(out=std_eps[s][:], in0=std[s][:], scalar1=EPS)
+            nc.vector.reciprocal(out=inv_std[s][:], in_=std_eps[s][:])
+            for h in range(BANKS):
+                cols = slice(BANK * h, BANK * (h + 1))
+                nc.vector.scalar_tensor_tensor(
+                    out=result[s][:, cols],
+                    in0=centred[s][:, cols],
+                    scalar=inv_std[s][:],
+                    in1=x_offset[s][:, cols],
+                    op0=ALU.mult,
+                    op1=ALU.add,
+                )
+                for p0, t0, count in token_runs(s):
+                    nc.sync.dma_start(
+                        out=out[0, t0 : t0 + count, cols], in_=result[s][p0 : p0 + count, cols]
+                    )

@@ -32,12 +32,11 @@ WARM = 4
 FLOPS = 2 * TOKENS * CHANNELS * CHANNELS
 
 
-def token_runs(s):
-    first = P * s + SHIFT * GRID
-    if first + P <= TOKENS:
-        return [(0, first, P)]
-    head = TOKENS - first
-    return [(0, first, head), (head, 0, P - head)]
+def tile_tokens(dram, s):
+    half = P // 2
+    if s == 0:
+        return dram[half : half + P, :]
+    return dram.rearrange("(q i) c -> i q c", i=half)[:, 0:4:3, :]
 
 
 def tile_swintransformerblock_pb_s_kernel(
@@ -100,20 +99,13 @@ def tile_swintransformerblock_pb_s_kernel(
         x_sb = one_per_tile(keep, [P, CHANNELS], BF16, "x_sb")
         gain_bf = one_per_tile(keep, [P, 1], BF16, "gain_bf")
         offset_bf = one_per_tile(keep, [P, 1], BF16, "offset_bf")
-        for s in tile_order:
-            for p0, t0, count in token_runs(s):
-                nc.sync.dma_start(out=x_sb[s][p0 : p0 + count, :], in_=x[0, t0 : t0 + count, :])
+        for s in reversed(tile_order):
+            nc.sync.dma_start(out=x_sb[s][:], in_=tile_tokens(x[0], s))
             with nc.allow_non_contiguous_dma(reason="one 2-byte value for each partition"):
-                for p0, t0, count in token_runs(s):
-                    nc.sync.dma_start(
-                        out=offset_bf[s][p0 : p0 + count, :], in_=ada1_shift[0, t0 : t0 + count, :]
-                    )
+                nc.sync.dma_start(out=offset_bf[s][:], in_=tile_tokens(ada1_shift[0], s))
         for s in tile_order:
             with nc.allow_non_contiguous_dma(reason="one 2-byte value for each partition"):
-                for p0, t0, count in token_runs(s):
-                    nc.sync.dma_start(
-                        out=gain_bf[s][p0 : p0 + count, :], in_=ada1_scale[0, t0 : t0 + count, :]
-                    )
+                nc.sync.dma_start(out=gain_bf[s][:], in_=tile_tokens(ada1_scale[0], s))
 
         ones = keep.tile([P, P], BF16)
         nc.vector.memset(ones[:], 1.0)
@@ -147,6 +139,13 @@ def tile_swintransformerblock_pb_s_kernel(
         a_words = per_pass(keep, [P, P], U32, "a_words", align_bytes=64)
         a_scales = per_pass(keep, [P, P], U8, "a_scales", align_bytes=64)
 
+        perm_wrapped = keep.tile([P, P], F32)
+        for half in range(2):
+            nc.vector.tensor_copy(
+                out=perm_wrapped[:, 1 - half : P : 2], in_=perm[:, half * P // 2 : (half + 1) * P // 2]
+            )
+        perms = [perm, perm_wrapped]
+
         def transpose_and_copy(s):
             o_pairs = o_sb[s][:].bitcast(F32)
             for g in range(PASSES):
@@ -154,7 +153,7 @@ def tile_swintransformerblock_pb_s_kernel(
                     nc.tensor.transpose(
                         transposed[s][g][:, u, :],
                         o_pairs[:, 2 * P * g + u : 2 * P * (g + 1) : 2],
-                        perm[:],
+                        perms[s][:],
                     )
             for g in range(PASSES):
                 nc.scalar.copy(
@@ -236,11 +235,33 @@ def tile_swintransformerblock_pb_s_kernel(
             op1=ALU.add,
         )
 
+        for s in tile_order:
+            nc.gpsimd.tensor_copy(out=gain[s][:], in_=gain_bf[s][:])
+
         neg_mean = one_per_tile(keep, [P, 1], F32, "neg_mean")
         squares = one_per_tile(keep, [P, CHANNELS], F32, "squares")
         sum_squares = one_per_tile(keep, [P, 1], F32, "sum_squares")
         centred = one_per_tile(keep, [P, CHANNELS], F32, "centred")
         std = one_per_tile(keep, [P, 1], F32, "std")
+        std_eps = one_per_tile(keep, [P, 1], F32, "std_eps")
+        inv_std = one_per_tile(keep, [P, 1], F32, "inv_std")
+
+        def centre(engine, s, cols):
+            engine.tensor_scalar(
+                out=centred[s][:, cols],
+                in0=a_sb[s][:, cols],
+                scalar1=neg_mean[s][:],
+                scalar2=gain[s][:],
+                op0=ALU.add,
+                op1=ALU.mult,
+            )
+
+        def add_eps(s):
+            nc.vector.tensor_scalar_add(out=std_eps[s][:], in0=std[s][:], scalar1=EPS)
+
+        def invert(s):
+            nc.vector.reciprocal(out=inv_std[s][:], in_=std_eps[s][:])
+
         for s in tile_order:
             for h in range(BANKS):
                 if (s, h) != (first, 0):
@@ -264,23 +285,21 @@ def tile_swintransformerblock_pb_s_kernel(
             nc.scalar.activation(
                 out=std[s][:], in_=sum_squares[s][:], func=ACT.Sqrt, scale=1.0 / (CHANNELS - 1)
             )
-            centring_engine = nc.gpsimd if s == tile_order[0] else nc.vector
-            centring_engine.tensor_copy(out=gain[s][:], in_=gain_bf[s][:])
-            centring_engine.tensor_scalar(
-                out=centred[s][:],
-                in0=a_sb[s][:],
-                scalar1=neg_mean[s][:],
-                scalar2=gain[s][:],
-                op0=ALU.add,
-                op1=ALU.mult,
-            )
+            if s == last:
+                add_eps(first)
+            if s == first:
+                centre(nc.gpsimd, s, slice(0, CHANNELS))
+            else:
+                centre(nc.vector, s, slice(0, BANK))
 
-        std_eps = one_per_tile(keep, [P, 1], F32, "std_eps")
-        inv_std = one_per_tile(keep, [P, 1], F32, "inv_std")
+        invert(first)
+
         result = one_per_tile(keep, [P, CHANNELS], F32, "result")
         for s in tile_order:
-            nc.vector.tensor_scalar_add(out=std_eps[s][:], in0=std[s][:], scalar1=EPS)
-            nc.vector.reciprocal(out=inv_std[s][:], in_=std_eps[s][:])
+            if s == last:
+                add_eps(s)
+                centre(nc.vector, s, slice(BANK, CHANNELS))
+                invert(s)
             for h in range(BANKS):
                 cols = slice(BANK * h, BANK * (h + 1))
                 nc.vector.scalar_tensor_tensor(
@@ -291,7 +310,4 @@ def tile_swintransformerblock_pb_s_kernel(
                     op0=ALU.mult,
                     op1=ALU.add,
                 )
-                for p0, t0, count in token_runs(s):
-                    nc.sync.dma_start(
-                        out=out[0, t0 : t0 + count, cols], in_=result[s][p0 : p0 + count, cols]
-                    )
+                nc.sync.dma_start(out=tile_tokens(out[0][:, cols], s), in_=result[s][:, cols])

@@ -57,7 +57,7 @@ def tile_swintransformerblock_pb_s_kernel(
         tile_order = [1, 0]
 
         warm_src = keep.tile([P, P], F32)
-        nc.vector.memset(warm_src[:], 1.0)
+        nc.gpsimd.memset(warm_src[:], 1.0)
         warm_ps = psum.tile([P, WARM, P], F32, name="warm_ps", tag="acc%d%d" % (tile_order[1], 0))
         for i in range(WARM):
             nc.tensor.matmul(

@@ -33,10 +33,7 @@ FLOPS = 2 * TOKENS * CHANNELS * CHANNELS
 
 
 def tile_tokens(dram, s):
-    half = P // 2
-    if s == 0:
-        return dram[half : half + P, :]
-    return dram.rearrange("(q i) c -> i q c", i=half)[:, 0:4:3, :]
+    return dram.rearrange("(p s) c -> s p c", s=TILES)[s]
 
 
 def tile_swintransformerblock_pb_s_kernel(
@@ -54,7 +51,8 @@ def tile_swintransformerblock_pb_s_kernel(
                 for s in range(TILES)
             ]
 
-        tile_order = [1, 0]
+        tile_order = [0, 1]
+        first, last = tile_order
 
         warm_src = keep.tile([P, P], F32)
         nc.gpsimd.memset(warm_src[:], 1.0)
@@ -71,7 +69,7 @@ def tile_swintransformerblock_pb_s_kernel(
         o_rows = o_attn.rearrange("w t c -> (w t) c")
         o_sb = one_per_tile(keep, [P, CHANNELS], BF16, "o_sb")
         for s in tile_order:
-            nc.sync.dma_start(out=o_sb[s][:], in_=o_rows[P * s : P * (s + 1), :])
+            nc.sync.dma_start(out=o_sb[s][:], in_=tile_tokens(o_rows, s))
 
         w_words = [
             keep.tile([P, PASSES, 2 * BANK], U8, name="w_words%d" % h, align_bytes=64)
@@ -97,15 +95,18 @@ def tile_swintransformerblock_pb_s_kernel(
         load_w_words(1)
 
         x_sb = one_per_tile(keep, [P, CHANNELS], BF16, "x_sb")
-        gain_bf = one_per_tile(keep, [P, 1], BF16, "gain_bf")
-        offset_bf = one_per_tile(keep, [P, 1], BF16, "offset_bf")
-        for s in reversed(tile_order):
-            nc.sync.dma_start(out=x_sb[s][:], in_=tile_tokens(x[0], s))
-            with nc.allow_non_contiguous_dma(reason="one 2-byte value for each partition"):
-                nc.sync.dma_start(out=offset_bf[s][:], in_=tile_tokens(ada1_shift[0], s))
-        for s in tile_order:
-            with nc.allow_non_contiguous_dma(reason="one 2-byte value for each partition"):
-                nc.sync.dma_start(out=gain_bf[s][:], in_=tile_tokens(ada1_scale[0], s))
+        gain_bf = keep.tile([P, TILES], BF16)
+        offset_bf = keep.tile([P, TILES], BF16)
+        with nc.allow_non_contiguous_dma(reason="two 2-byte values for each partition"):
+            nc.sync.dma_start(
+                out=offset_bf[:], in_=ada1_shift[0].rearrange("(p s) o -> p (s o)", s=TILES)
+            )
+        with nc.allow_non_contiguous_dma(reason="two 2-byte values for each partition"):
+            nc.sync.dma_start(
+                out=gain_bf[:], in_=ada1_scale[0].rearrange("(p s) o -> p (s o)", s=TILES)
+            )
+        nc.sync.dma_start(out=x_sb[first][:], in_=tile_tokens(x[0], first))
+        nc.sync.dma_start(out=x_sb[last][:], in_=tile_tokens(x[0], last))
 
         ones = keep.tile([P, P], BF16)
         nc.vector.memset(ones[:], 1.0)
@@ -117,13 +118,17 @@ def tile_swintransformerblock_pb_s_kernel(
         ident = keep.tile([P, P], F32)
         make_identity(nc, ident[:])
         perm = keep.tile([P, P], F32)
-        by_window = ident[:].rearrange("p (wj r c) -> p wj r c", wj=2, r=WIN)
-        by_image_row = perm[:].rearrange("p (r j) -> p r j", j=GRID)
-        nc.vector.tensor_copy(out=by_image_row[:, :, SHIFT : SHIFT + WIN], in_=by_window[:, 0, :, :])
-        nc.vector.tensor_copy(
-            out=by_image_row[:, :, SHIFT + WIN : GRID], in_=by_window[:, 1, :, 0 : WIN - SHIFT]
-        )
-        nc.vector.tensor_copy(out=by_image_row[:, :, 0:SHIFT], in_=by_window[:, 1, :, WIN - SHIFT : WIN])
+        by_window = ident[:].rearrange("p (w v h r c) -> p w v h r c", w=2, v=2, h=2, r=4)
+        by_image_row = perm[:].rearrange("p (q r j) -> p q r j", q=4, r=4)
+        for v, c0, j0, count in [(0, 0, 2, 4), (1, 0, 6, 2), (1, 2, 0, 2)]:
+            nc.vector.tensor_copy(
+                out=by_image_row[:, 1:3, :, j0 : j0 + count],
+                in_=by_window[:, 0, v, :, :, c0 : c0 + count],
+            )
+            nc.vector.tensor_copy(
+                out=by_image_row[:, 0:4:3, :, j0 : j0 + count],
+                in_=by_window[:, 1, v, ::-1, :, c0 : c0 + count],
+            )
 
         def per_pass(pool, shape, dtype, name, align_bytes=None):
             return [
@@ -139,13 +144,6 @@ def tile_swintransformerblock_pb_s_kernel(
         a_words = per_pass(keep, [P, P], U32, "a_words", align_bytes=64)
         a_scales = per_pass(keep, [P, P], U8, "a_scales", align_bytes=64)
 
-        perm_wrapped = keep.tile([P, P], F32)
-        for half in range(2):
-            nc.vector.tensor_copy(
-                out=perm_wrapped[:, 1 - half : P : 2], in_=perm[:, half * P // 2 : (half + 1) * P // 2]
-            )
-        perms = [perm, perm_wrapped]
-
         def transpose_and_copy(s):
             o_pairs = o_sb[s][:].bitcast(F32)
             for g in range(PASSES):
@@ -153,7 +151,7 @@ def tile_swintransformerblock_pb_s_kernel(
                     nc.tensor.transpose(
                         transposed[s][g][:, u, :],
                         o_pairs[:, 2 * P * g + u : 2 * P * (g + 1) : 2],
-                        perms[s][:],
+                        perm[:],
                     )
             for g in range(PASSES):
                 nc.scalar.copy(
@@ -196,7 +194,6 @@ def tile_swintransformerblock_pb_s_kernel(
                 accum_out=row_sums[s][:, h : h + 1],
             )
 
-        first, last = tile_order
         transpose_and_copy(first)
         bias_ps = psum.tile([P, CHANNELS], BF16, name="bias_ps", tag="acc%d%d" % (last, BANKS - 1))
         for h in range(BANKS):
@@ -211,32 +208,34 @@ def tile_swintransformerblock_pb_s_kernel(
         nc.vector.tensor_copy(out=bias_all[:], in_=bias_ps[:])
         quantise(last, 0)
         project(first, 0)
-        add_bias(first, 0)
         quantise(last, 1)
+        add_bias(first, 0)
         project(first, 1)
         project(last, 0)
         project(last, 1)
 
-        x_offset = one_per_tile(keep, [P, CHANNELS], F32, "x_offset")
-        gain = one_per_tile(keep, [P, 1], F32, "gain")
-        nc.scalar.activation(
-            out=x_offset[tile_order[0]][:],
-            in_=x_sb[tile_order[0]][:],
-            func=ACT.Identity,
-            bias=offset_bf[tile_order[0]][:],
-            scale=1.0,
-        )
+        offset = keep.tile([P, 1], F32)
+        nc.gpsimd.tensor_copy(out=offset[:], in_=offset_bf[:, last : last + 1])
+        eps_offset = keep.tile([P, 1], F32)
         nc.gpsimd.tensor_scalar(
-            out=x_offset[tile_order[1]][:],
-            in0=x_sb[tile_order[1]][:],
-            scalar1=1.0,
-            scalar2=offset_bf[tile_order[1]][:],
+            out=eps_offset[:],
+            in0=offset_bf[:, last : last + 1],
+            scalar1=EPS,
+            scalar2=0.0,
             op0=ALU.mult,
             op1=ALU.add,
         )
-
-        for s in tile_order:
-            nc.gpsimd.tensor_copy(out=gain[s][:], in_=gain_bf[s][:])
+        gain = keep.tile([P, TILES], F32)
+        nc.gpsimd.tensor_copy(out=gain[:], in_=gain_bf[:])
+        x_offset = keep.tile([P, CHANNELS], F32)
+        nc.gpsimd.tensor_scalar(
+            out=x_offset[:],
+            in0=x_sb[first][:],
+            scalar1=1.0,
+            scalar2=offset_bf[:, first : first + 1],
+            op0=ALU.mult,
+            op1=ALU.add,
+        )
 
         neg_mean = one_per_tile(keep, [P, 1], F32, "neg_mean")
         squares = one_per_tile(keep, [P, CHANNELS], F32, "squares")
@@ -245,27 +244,10 @@ def tile_swintransformerblock_pb_s_kernel(
         std = one_per_tile(keep, [P, 1], F32, "std")
         std_eps = one_per_tile(keep, [P, 1], F32, "std_eps")
         inv_std = one_per_tile(keep, [P, 1], F32, "inv_std")
+        shift_base = keep.tile([P, 1], F32)
+        shift = keep.tile([P, 1], F32)
 
-        def centre(engine, s, cols):
-            engine.tensor_scalar(
-                out=centred[s][:, cols],
-                in0=a_sb[s][:, cols],
-                scalar1=neg_mean[s][:],
-                scalar2=gain[s][:],
-                op0=ALU.add,
-                op1=ALU.mult,
-            )
-
-        def add_eps(s):
-            nc.vector.tensor_scalar_add(out=std_eps[s][:], in0=std[s][:], scalar1=EPS)
-
-        def invert(s):
-            nc.vector.reciprocal(out=inv_std[s][:], in_=std_eps[s][:])
-
-        for s in tile_order:
-            for h in range(BANKS):
-                if (s, h) != (first, 0):
-                    add_bias(s, h)
+        def statistics(s):
             nc.vector.tensor_scalar(
                 out=neg_mean[s][:],
                 in0=row_sums[s][:, 0:1],
@@ -285,29 +267,72 @@ def tile_swintransformerblock_pb_s_kernel(
             nc.scalar.activation(
                 out=std[s][:], in_=sum_squares[s][:], func=ACT.Sqrt, scale=1.0 / (CHANNELS - 1)
             )
-            if s == last:
-                add_eps(first)
-            if s == first:
-                centre(nc.gpsimd, s, slice(0, CHANNELS))
-            else:
-                centre(nc.vector, s, slice(0, BANK))
 
-        invert(first)
+        def add_eps(s):
+            nc.vector.tensor_scalar_add(out=std_eps[s][:], in0=std[s][:], scalar1=EPS)
+
+        def invert(s):
+            nc.vector.reciprocal(out=inv_std[s][:], in_=std_eps[s][:])
 
         result = one_per_tile(keep, [P, CHANNELS], F32, "result")
-        for s in tile_order:
-            if s == last:
-                add_eps(s)
-                centre(nc.vector, s, slice(BANK, CHANNELS))
-                invert(s)
-            for h in range(BANKS):
-                cols = slice(BANK * h, BANK * (h + 1))
-                nc.vector.scalar_tensor_tensor(
-                    out=result[s][:, cols],
-                    in0=centred[s][:, cols],
-                    scalar=inv_std[s][:],
-                    in1=x_offset[s][:, cols],
-                    op0=ALU.mult,
-                    op1=ALU.add,
-                )
-                nc.sync.dma_start(out=tile_tokens(out[0][:, cols], s), in_=result[s][:, cols])
+
+        def finish(s, h, residual):
+            cols = slice(BANK * h, BANK * (h + 1))
+            nc.vector.scalar_tensor_tensor(
+                out=result[s][:, cols],
+                in0=centred[s][:, cols],
+                scalar=inv_std[s][:],
+                in1=residual[:, cols],
+                op0=ALU.mult,
+                op1=ALU.add,
+            )
+            nc.sync.dma_start(out=tile_tokens(out[0][:, cols], s), in_=result[s][:, cols])
+
+        add_bias(first, 1)
+        statistics(first)
+        nc.gpsimd.tensor_scalar(
+            out=centred[first][:],
+            in0=a_sb[first][:],
+            scalar1=neg_mean[first][:],
+            scalar2=gain[:, first : first + 1],
+            op0=ALU.add,
+            op1=ALU.mult,
+        )
+        add_bias(last, 0)
+        add_bias(last, 1)
+        statistics(last)
+        nc.gpsimd.tensor_scalar(
+            out=shift_base[:],
+            in0=neg_mean[last][:],
+            scalar1=gain[:, last : last + 1],
+            scalar2=eps_offset[:],
+            op0=ALU.mult,
+            op1=ALU.add,
+        )
+        nc.scalar.activation(
+            out=shift[:], in_=std[last][:], func=ACT.Identity, bias=shift_base[:], scale=offset[:]
+        )
+
+        add_eps(first)
+        invert(first)
+        for h in range(BANKS):
+            finish(first, h, x_offset)
+        add_eps(last)
+        nc.vector.tensor_scalar(
+            out=centred[last][:, 0:BANK],
+            in0=a_sb[last][:, 0:BANK],
+            scalar1=gain[:, last : last + 1],
+            scalar2=shift[:],
+            op0=ALU.mult,
+            op1=ALU.add,
+        )
+        nc.scalar.activation(
+            out=centred[last][:, BANK:CHANNELS],
+            in_=a_sb[last][:, BANK:CHANNELS],
+            func=ACT.Identity,
+            bias=shift[:],
+            scale=gain[:, last : last + 1],
+        )
+        invert(last)
+        for h in range(BANKS):
+            finish(last, h, x_sb[last])

@@ -276,8 +276,7 @@ def tile_swintransformerblock_pb_s_kernel(
 
         result = one_per_tile(keep, [P, CHANNELS], F32, "result")
 
-        def finish(s, h, residual):
-            cols = slice(BANK * h, BANK * (h + 1))
+        def finish(s, cols, residual):
             nc.vector.scalar_tensor_tensor(
                 out=result[s][:, cols],
                 in0=centred[s][:, cols],
@@ -315,8 +314,7 @@ def tile_swintransformerblock_pb_s_kernel(
 
         add_eps(first)
         invert(first)
-        for h in range(BANKS):
-            finish(first, h, x_offset)
+        finish(first, slice(0, CHANNELS), x_offset)
         add_eps(last)
         nc.vector.tensor_scalar(
             out=centred[last][:, 0:BANK],
@@ -335,4 +333,4 @@ def tile_swintransformerblock_pb_s_kernel(
         )
         invert(last)
         for h in range(BANKS):
-            finish(last, h, x_sb[last])
+            finish(last, slice(BANK * h, BANK * (h + 1)), x_sb[last])

@@ -54,6 +54,8 @@ def tile_swintransformerblock_pb_s_kernel(
         tile_order = [0, 1]
         first, last = tile_order
 
+        one_col = keep.tile([P, 1], F32)
+        nc.gpsimd.memset(one_col[:], 1.0)
         warm_src = keep.tile([P, P], F32)
         nc.gpsimd.memset(warm_src[:], 1.0)
         warm_ps = psum.tile([P, WARM, P], F32, name="warm_ps", tag="acc%d%d" % (tile_order[1], 0))
@@ -62,9 +64,11 @@ def tile_swintransformerblock_pb_s_kernel(
                 out=warm_ps[:, i, :], lhsT=warm_src[:], rhs=warm_src[:], start=True, stop=True
             )
 
-        bias_rows = keep.tile([P, CHANNELS], BF16)
+        bias_rows = keep.tile([P, BANK], BF16)
         nc.vector.memset(bias_rows[:].bitcast(I32), 0)
-        nc.scalar.dma_start(out=bias_rows[0:1, :], in_=out_b.rearrange("(o c) -> o c", o=1))
+        nc.scalar.dma_start(
+            out=bias_rows[0 : 32 * BANKS : 32, :], in_=out_b.rearrange("(h c) -> h c", h=BANKS)
+        )
 
         o_rows = o_attn.rearrange("w t c -> (w t) c")
         o_sb = one_per_tile(keep, [P, CHANNELS], BF16, "o_sb")
@@ -108,10 +112,10 @@ def tile_swintransformerblock_pb_s_kernel(
         nc.sync.dma_start(out=x_sb[first][:], in_=tile_tokens(x[0], first))
         nc.sync.dma_start(out=x_sb[last][:], in_=tile_tokens(x[0], last))
 
-        ones = keep.tile([P, P], BF16)
-        nc.vector.memset(ones[:], 1.0)
-        one_col = keep.tile([P, 1], F32)
-        nc.vector.memset(one_col[:], 1.0)
+        pick_row = keep.tile([P, BANKS, P], BF16)
+        nc.vector.memset(pick_row[:].rearrange("p h m -> p (h m)").bitcast(I32), 0)
+        for h in range(BANKS):
+            nc.vector.memset(pick_row[32 * h : 32 * h + 1, h, :], 1.0)
         sqrt_warm = keep.tile([P, 1], F32)
         nc.scalar.activation(out=sqrt_warm[:], in_=one_col[:], func=ACT.Sqrt)
 
@@ -199,7 +203,7 @@ def tile_swintransformerblock_pb_s_kernel(
         for h in range(BANKS):
             cols = slice(BANK * h, BANK * (h + 1))
             nc.tensor.matmul(
-                out=bias_ps[:, cols], lhsT=ones[:], rhs=bias_rows[:, cols], start=True, stop=True
+                out=bias_ps[:, cols], lhsT=pick_row[:, h, :], rhs=bias_rows[:], start=True, stop=True
             )
         transpose_and_copy(last)
         quantise(first, 0)

@@ -27,7 +27,7 @@ PASSES = CHANNELS // K_PASS
 BANK = 512
 BANKS = CHANNELS // BANK
 
-WARM = 4
+WARM = 3
 
 FLOPS = 2 * TOKENS * CHANNELS * CHANNELS
 

@@ -27,6 +27,9 @@ PASSES = CHANNELS // K_PASS
 BANK = 512
 BANKS = CHANNELS // BANK
 
+BIAS_ROWS = 4
+QUARTER = CHANNELS // BIAS_ROWS
+
 WARM = 3
 
 FLOPS = 2 * TOKENS * CHANNELS * CHANNELS
@@ -54,6 +57,9 @@ def tile_swintransformerblock_pb_s_kernel(
         tile_order = [0, 1]
         first, last = tile_order
 
+        bias_rows = keep.tile([P, QUARTER], BF16)
+        nc.gpsimd.memset(bias_rows[:].bitcast(I32), 0)
+
         one_col = keep.tile([P, 1], F32)
         nc.gpsimd.memset(one_col[:], 1.0)
         warm_src = keep.tile([P, P], F32)
@@ -64,11 +70,7 @@ def tile_swintransformerblock_pb_s_kernel(
                 out=warm_ps[:, i, :], lhsT=warm_src[:], rhs=warm_src[:], start=True, stop=True
             )
 
-        bias_rows = keep.tile([P, BANK], BF16)
-        nc.vector.memset(bias_rows[:].bitcast(I32), 0)
-        nc.scalar.dma_start(
-            out=bias_rows[0 : 32 * BANKS : 32, :], in_=out_b.rearrange("(h c) -> h c", h=BANKS)
-        )
+        nc.scalar.dma_start(out=bias_rows[0:P:32, :], in_=out_b.rearrange("(q c) -> q c", q=BIAS_ROWS))
 
         o_rows = o_attn.rearrange("w t c -> (w t) c")
         o_sb = one_per_tile(keep, [P, CHANNELS], BF16, "o_sb")
@@ -112,10 +114,6 @@ def tile_swintransformerblock_pb_s_kernel(
         nc.sync.dma_start(out=x_sb[first][:], in_=tile_tokens(x[0], first))
         nc.sync.dma_start(out=x_sb[last][:], in_=tile_tokens(x[0], last))
 
-        pick_row = keep.tile([P, BANKS, P], BF16)
-        nc.vector.memset(pick_row[:].rearrange("p h m -> p (h m)").bitcast(I32), 0)
-        for h in range(BANKS):
-            nc.vector.memset(pick_row[32 * h : 32 * h + 1, h, :], 1.0)
         sqrt_warm = keep.tile([P, 1], F32)
         nc.scalar.activation(out=sqrt_warm[:], in_=one_col[:], func=ACT.Sqrt)
 
@@ -133,6 +131,11 @@ def tile_swintransformerblock_pb_s_kernel(
                 out=by_image_row[:, 0:4:3, :, j0 : j0 + count],
                 in_=by_window[:, 1, v, ::-1, :, c0 : c0 + count],
             )
+
+        pick_row = keep.tile([P, BIAS_ROWS, P], BF16)
+        nc.vector.memset(pick_row[:].rearrange("p q m -> p (q m)").bitcast(I32), 0)
+        for q in range(BIAS_ROWS):
+            nc.vector.memset(pick_row[32 * q : 32 * q + 1, q, :], 1.0)
 
         def per_pass(pool, shape, dtype, name, align_bytes=None):
             return [
@@ -200,10 +203,10 @@ def tile_swintransformerblock_pb_s_kernel(
 
         transpose_and_copy(first)
         bias_ps = psum.tile([P, CHANNELS], BF16, name="bias_ps", tag="acc%d%d" % (last, BANKS - 1))
-        for h in range(BANKS):
-            cols = slice(BANK * h, BANK * (h + 1))
+        for q in range(BIAS_ROWS):
+            cols = slice(QUARTER * q, QUARTER * (q + 1))
             nc.tensor.matmul(
-                out=bias_ps[:, cols], lhsT=pick_row[:, h, :], rhs=bias_rows[:], start=True, stop=True
+                out=bias_ps[:, cols], lhsT=pick_row[:, q, :], rhs=bias_rows[:], start=True, stop=True
             )
         transpose_and_copy(last)
         quantise(first, 0)

from contextlib import ExitStack

import concourse.mybir as mybir
from concourse.masks import make_identity

F32 = mybir.dt.float32
BF16 = mybir.dt.bfloat16
I32 = mybir.dt.int32
U32 = mybir.dt.uint32
U8 = mybir.dt.uint8
FP8X4 = mybir.dt.float8_e4m3fn_x4
FP4X4 = mybir.dt.float4_e2m1fn_x4
ALU = mybir.AluOpType
ACT = mybir.ActivationFunctionType

P = 128
GRID = 16
WIN = 8
SHIFT = 4
TOKENS = GRID * GRID
CHANNELS = 1024
EPS = 1e-5

TILES = TOKENS // P
K_PASS = 4 * P
PASSES = CHANNELS // K_PASS
BANK = 512
BANKS = CHANNELS // BANK

BIAS_ROWS = 4
QUARTER = CHANNELS // BIAS_ROWS

WARM = 3

FLOPS = 2 * TOKENS * CHANNELS * CHANNELS


def tile_tokens(dram, s):
    return dram.rearrange("(p s) c -> s p c", s=TILES)[s]


def tile_swintransformerblock_pb_s_kernel(
    tc, o_attn, out_w_words, out_w_scales, out_b, ada1_scale, ada1_shift, x, out
):
    nc = tc.nc
    with ExitStack() as ctx:
        keep = ctx.enter_context(tc.tile_pool(name="keep", bufs=1))
        psum = ctx.enter_context(tc.psum_pool(name="psum", bufs=1))
        ctx.enter_context(tc.manual_schedule())

        def one_per_tile(pool, shape, dtype, name, align_bytes=None):
            return [
                pool.tile(shape, dtype, name="%s%d" % (name, s), align_bytes=align_bytes)
                for s in range(TILES)
            ]

        tile_order = [0, 1]
        first, last = tile_order

        bias_rows = keep.tile([P, QUARTER], BF16)
        nc.gpsimd.memset(bias_rows[:].bitcast(I32), 0)

        one_col = keep.tile([P, 1], F32)
        nc.gpsimd.memset(one_col[:], 1.0)
        warm_src = keep.tile([P, P], F32)
        nc.gpsimd.memset(warm_src[:], 1.0)
        warm_ps = psum.tile([P, WARM, P], F32, name="warm_ps", tag="acc%d%d" % (tile_order[1], 0))
        for i in range(WARM):
            nc.tensor.matmul(
                out=warm_ps[:, i, :], lhsT=warm_src[:], rhs=warm_src[:], start=True, stop=True
            )

        nc.scalar.dma_start(out=bias_rows[0:P:32, :], in_=out_b.rearrange("(q c) -> q c", q=BIAS_ROWS))

        o_rows = o_attn.rearrange("w t c -> (w t) c")
        o_sb = one_per_tile(keep, [P, CHANNELS], BF16, "o_sb")
        for s in tile_order:
            nc.sync.dma_start(out=o_sb[s][:], in_=tile_tokens(o_rows, s))

        w_words = [
            keep.tile([P, PASSES, 2 * BANK], U8, name="w_words%d" % h, align_bytes=64)
            for h in range(BANKS)
        ]

        def load_w_words(h):
            nc.sync.dma_start(
                out=w_words[h][:].bitcast(I32),
                in_=out_w_words.rearrange("g p b -> p g b")[
                    :, :, 2 * BANK * h : 2 * BANK * (h + 1)
                ].bitcast(I32),
            )

        w_scales = keep.tile([P, PASSES, CHANNELS], U8, align_bytes=64)
        nc.vector.memset(w_scales[:].bitcast(I32), 0)
        for r in range(4):
            nc.sync.dma_start(
                out=w_scales[r:P:32, :, :].bitcast(I32),
                in_=out_w_scales[:, r:16:4, :].rearrange("g q n -> q g n").bitcast(I32),
            )
        load_w_words(0)
        load_w_words(1)

        x_sb = one_per_tile(keep, [P, CHANNELS], BF16, "x_sb")
        gain_bf = keep.tile([P, TILES], BF16)
        offset_bf = keep.tile([P, TILES], BF16)
        with nc.allow_non_contiguous_dma(reason="two 2-byte values for each partition"):
            nc.sync.dma_start(
                out=offset_bf[:], in_=ada1_shift[0].rearrange("(p s) o -> p (s o)", s=TILES)
            )
        with nc.allow_non_contiguous_dma(reason="two 2-byte values for each partition"):
            nc.sync.dma_start(
                out=gain_bf[:], in_=ada1_scale[0].rearrange("(p s) o -> p (s o)", s=TILES)
            )
        nc.sync.dma_start(out=x_sb[first][:], in_=tile_tokens(x[0], first))
        nc.sync.dma_start(out=x_sb[last][:], in_=tile_tokens(x[0], last))

        sqrt_warm = keep.tile([P, 1], F32)
        nc.scalar.activation(out=sqrt_warm[:], in_=one_col[:], func=ACT.Sqrt)

        ident = keep.tile([P, P], F32)
        make_identity(nc, ident[:])
        perm = keep.tile([P, P], F32)
        by_window = ident[:].rearrange("p (w v h r c) -> p w v h r c", w=2, v=2, h=2, r=4)
        by_image_row = perm[:].rearrange("p (q r j) -> p q r j", q=4, r=4)
        for v, c0, j0, count in [(0, 0, 2, 4), (1, 0, 6, 2), (1, 2, 0, 2)]:
            nc.vector.tensor_copy(
                out=by_image_row[:, 1:3, :, j0 : j0 + count],
                in_=by_window[:, 0, v, :, :, c0 : c0 + count],
            )
            nc.vector.tensor_copy(
                out=by_image_row[:, 0:4:3, :, j0 : j0 + count],
                in_=by_window[:, 1, v, ::-1, :, c0 : c0 + count],
            )

        pick_row = keep.tile([P, BIAS_ROWS, P], BF16)
        nc.vector.memset(pick_row[:].rearrange("p q m -> p (q m)").bitcast(I32), 0)
        for q in range(BIAS_ROWS):
            nc.vector.memset(pick_row[32 * q : 32 * q + 1, q, :], 1.0)

        def per_pass(pool, shape, dtype, name, align_bytes=None):
            return [
                [
                    pool.tile(shape, dtype, name="%s%d%d" % (name, s, g), align_bytes=align_bytes)
                    for g in range(PASSES)
                ]
                for s in range(TILES)
            ]

        transposed = per_pass(psum, [P, 4, P], F32, "transposed")
        grouped = per_pass(keep, [P, P * 4], BF16, "grouped", align_bytes=64)
        a_words = per_pass(keep, [P, P], U32, "a_words", align_bytes=64)
        a_scales = per_pass(keep, [P, P], U8, "a_scales", align_bytes=64)

        def transpose_and_copy(s):
            o_pairs = o_sb[s][:].bitcast(F32)
            for g in range(PASSES):
                for u in range(2):
                    nc.tensor.transpose(
                        transposed[s][g][:, u, :],
                        o_pairs[:, 2 * P * g + u : 2 * P * (g + 1) : 2],
                        perm[:],
                    )
            for g in range(PASSES):
                nc.scalar.copy(
                    out=grouped[s][g][:].bitcast(F32).rearrange("p (n u) -> p n u", u=2),
                    in_=transposed[s][g][:, 0:2, :].rearrange("p u n -> p n u"),
                )

        def quantise(s, g):
            nc.vector.quantize_mx(
                out=a_words[s][g][:].bitcast(FP8X4), scales=a_scales[s][g][:], in_=grouped[s][g][:]
            )

        acc = [[None for h in range(BANKS)] for s in range(TILES)]

        def project(s, h):
            acc[s][h] = psum.tile([P, BANK], F32, name="acc%d%d" % (s, h), tag="acc%d%d" % (s, h))
            for g in range(PASSES):
                nc.tensor.matmul_mx(
                    out=acc[s][h][:],
                    lhsT=a_words[s][g][:].bitcast(FP8X4),
                    lhsT_scale=a_scales[s][g][:],
                    rhs=w_words[h][:, g, :].bitcast(FP4X4),
                    rhs_scale=w_scales[:, g, BANK * h : BANK * (h + 1)],
                    start=(g == 0),
                    stop=(g == PASSES - 1),
                )

        a_sb = one_per_tile(keep, [P, CHANNELS], F32, "a_sb")
        row_sums = one_per_tile(keep, [P, BANKS], F32, "row_sums")

        def add_bias(s, h):
            cols = slice(BANK * h, BANK * (h + 1))
            nc.vector.scalar_tensor_tensor(
                out=a_sb[s][:, cols],
                in0=acc[s][h][:],
                scalar=1.0,
                in1=bias_all[:, cols],
                op0=ALU.mult,
                op1=ALU.add,
                accum_out=row_sums[s][:, h : h + 1],
            )

        transpose_and_copy(first)
        bias_ps = psum.tile([P, CHANNELS], BF16, name="bias_ps", tag="acc%d%d" % (last, BANKS - 1))
        for q in range(BIAS_ROWS):
            cols = slice(QUARTER * q, QUARTER * (q + 1))
            nc.tensor.matmul(
                out=bias_ps[:, cols], lhsT=pick_row[:, q, :], rhs=bias_rows[:], start=True, stop=True
            )
        transpose_and_copy(last)
        quantise(first, 0)
        quantise(first, 1)
        bias_all = keep.tile([P, CHANNELS], BF16)
        nc.vector.tensor_copy(out=bias_all[:], in_=bias_ps[:])
        quantise(last, 0)
        project(first, 0)
        quantise(last, 1)
        add_bias(first, 0)
        project(first, 1)
        project(last, 0)
        project(last, 1)

        offset = keep.tile([P, 1], F32)
        nc.gpsimd.tensor_copy(out=offset[:], in_=offset_bf[:, last : last + 1])
        eps_offset = keep.tile([P, 1], F32)
        nc.gpsimd.tensor_scalar(
            out=eps_offset[:],
            in0=offset_bf[:, last : last + 1],
            scalar1=EPS,
            scalar2=0.0,
            op0=ALU.mult,
            op1=ALU.add,
        )
        gain = keep.tile([P, TILES], F32)
        nc.gpsimd.tensor_copy(out=gain[:], in_=gain_bf[:])
        x_offset = keep.tile([P, CHANNELS], F32)
        nc.gpsimd.tensor_scalar(
            out=x_offset[:],
            in0=x_sb[first][:],
            scalar1=1.0,
            scalar2=offset_bf[:, first : first + 1],
            op0=ALU.mult,
            op1=ALU.add,
        )

        neg_mean = one_per_tile(keep, [P, 1], F32, "neg_mean")
        squares = one_per_tile(keep, [P, CHANNELS], F32, "squares")
        sum_squares = one_per_tile(keep, [P, 1], F32, "sum_squares")
        centred = one_per_tile(keep, [P, CHANNELS], F32, "centred")
        std = one_per_tile(keep, [P, 1], F32, "std")
        std_eps = one_per_tile(keep, [P, 1], F32, "std_eps")
        inv_std = one_per_tile(keep, [P, 1], F32, "inv_std")
        shift_base = keep.tile([P, 1], F32)
        shift = keep.tile([P, 1], F32)

        def statistics(s):
            nc.vector.tensor_scalar(
                out=neg_mean[s][:],
                in0=row_sums[s][:, 0:1],
                scalar1=row_sums[s][:, 1:2],
                scalar2=-1.0 / CHANNELS,
                op0=ALU.add,
                op1=ALU.mult,
            )
            nc.scalar.activation(
                out=squares[s][:],
                in_=a_sb[s][:],
                func=ACT.Square,
                bias=neg_mean[s][:],
                scale=1.0,
                accum_out=sum_squares[s][:],
            )
            nc.scalar.activation(
                out=std[s][:], in_=sum_squares[s][:], func=ACT.Sqrt, scale=1.0 / (CHANNELS - 1)
            )

        def add_eps(s):
            nc.vector.tensor_scalar_add(out=std_eps[s][:], in0=std[s][:], scalar1=EPS)

        def invert(s):
            nc.vector.reciprocal(out=inv_std[s][:], in_=std_eps[s][:])

        result = one_per_tile(keep, [P, CHANNELS], F32, "result")

        def finish(s, cols, residual):
            nc.vector.scalar_tensor_tensor(
                out=result[s][:, cols],
                in0=centred[s][:, cols],
                scalar=inv_std[s][:],
                in1=residual[:, cols],
                op0=ALU.mult,
                op1=ALU.add,
            )
            nc.sync.dma_start(out=tile_tokens(out[0][:, cols], s), in_=result[s][:, cols])

        add_bias(first, 1)
        statistics(first)
        nc.gpsimd.tensor_scalar(
            out=centred[first][:],
            in0=a_sb[first][:],
            scalar1=neg_mean[first][:],
            scalar2=gain[:, first : first + 1],
            op0=ALU.add,
            op1=ALU.mult,
        )
        add_bias(last, 0)
        add_bias(last, 1)
        statistics(last)
        nc.gpsimd.tensor_scalar(
            out=shift_base[:],
            in0=neg_mean[last][:],
            scalar1=gain[:, last : last + 1],
            scalar2=eps_offset[:],
            op0=ALU.mult,
            op1=ALU.add,
        )
        nc.scalar.activation(
            out=shift[:], in_=std[last][:], func=ACT.Identity, bias=shift_base[:], scale=offset[:]
        )

        add_eps(first)
        invert(first)
        finish(first, slice(0, CHANNELS), x_offset)
        add_eps(last)
        nc.vector.tensor_scalar(
            out=centred[last][:, 0:BANK],
            in0=a_sb[last][:, 0:BANK],
            scalar1=gain[:, last : last + 1],
            scalar2=shift[:],
            op0=ALU.mult,
            op1=ALU.add,
        )
        nc.scalar.activation(
            out=centred[last][:, BANK:CHANNELS],
            in_=a_sb[last][:, BANK:CHANNELS],
            func=ACT.Identity,
            bias=shift[:],
            scale=gain[:, last : last + 1],
        )
        invert(last)
        for h in range(BANKS):
            finish(last, slice(BANK * h, BANK * (h + 1)), x_sb[last])
